import numpy as np
import ml_dtypes

BF16 = ml_dtypes.bfloat16


def bf(x):
    return np.asarray(x, np.float32).astype(BF16)


def f32(x):
    return np.asarray(x, np.float32)


def f64(x):
    return np.asarray(x).astype(np.float64)


def striped(idx):
    return np.tile(idx.reshape(-1, 16).T, (8, 1))


C, S, T, L, N = 256, 256, 32, 16, 512
EPS = 1e-5


def setup_inputs():
    return {"h": f32(np.random.standard_normal((C, S))), "gain": f32(1.0 + 0.1 * np.random.standard_normal((C, 1))), "beta": f32(0.1 * np.random.standard_normal((C, 1))), "att": f32(np.random.standard_normal((1, N))), "offs": striped(np.random.permutation(np.tile(np.arange(S), 2))[:N])}


def reference(h, gain, beta, att, offs):
    idx = offs[:16].T.reshape(-1)
    r = np.maximum(f64(h), 0.0)
    mu = r.mean(axis=1, keepdims=True)
    var = np.square(r - mu).mean(axis=1, keepdims=True)
    y = (r - mu) / np.sqrt(var + EPS) * f64(gain) + f64(beta)
    e = np.exp(f64(att)).reshape(T, L)
    a = (e / e.sum(axis=1, keepdims=True)).reshape(1, N)
    return (y[:, idx] * a).reshape(C, T, L).sum(axis=2)

@@ -1,0 +1,180 @@
+import concourse.mybir as mybir
+from concourse.masks import make_identity
+
+F32 = mybir.dt.float32
+U16 = mybir.dt.uint16
+ALU = mybir.AluOpType
+ACT = mybir.ActivationFunctionType
+AXIS = mybir.AxisListType
+
+P = 128
+C, S, T, L, N = 256, 256, 32, 16, 512
+EPS = 1e-5
+BLOCKS = C // P
+PIECE = S
+PIECES = N // PIECE
+PIECE_TEAMS = PIECE // L
+W_PIECE = 128
+W_TEAMS = W_PIECE // L
+BY_TEAM = "p (t l) -> p t l"
+
+
+def tile_tag_kernel(tc, h, gain, beta, att, offs, out):
+    nc = tc.nc
+    with (
+        tc.tile_pool(name="held", bufs=1) as held,
+        tc.psum_pool(name="psum", bufs=1) as psum,
+    ):
+        offsets = held.tile([P, N // 16], U16, name="offsets")
+        scores = held.tile([P, N], F32, name="scores")
+        nc.sync.dma_start(scores[:], att.broadcast_to([P, N]))
+        raw = [held.tile([P, S], F32, name=f"raw{b}") for b in range(BLOCKS)]
+        for b in range(BLOCKS):
+            nc.sync.dma_start(raw[b][:], h.rearrange("(p b) s -> b p s", b=BLOCKS)[b])
+        nc.sync.dma_start(offsets[:], offs)
+        team_scores = held.tile([T, L], F32, name="team_scores")
+        nc.sync.dma_start(team_scores[:], att.rearrange("o (t l) -> (o t) l", l=L))
+        gains = held.tile([P, BLOCKS], F32, name="gains")
+        betas = held.tile([P, BLOCKS], F32, name="betas")
+        nc.sync.dma_start(gains[:], gain.rearrange("(p b) o -> p (b o)", b=BLOCKS))
+        nc.sync.dma_start(betas[:], beta.rearrange("(p b) o -> p (b o)", b=BLOCKS))
+
+        minus_gains = held.tile([P, BLOCKS], F32, name="minus_gains")
+        nc.gpsimd.tensor_scalar(
+            out=minus_gains[:], in0=gains[:], scalar1=-1.0, scalar2=None, op0=ALU.mult
+        )
+
+        minus_half = held.tile([P, BLOCKS], F32, name="minus_half")
+        nc.gpsimd.memset(minus_half[:], -0.5)
+        eps = held.tile([P, 1], F32, name="eps")
+        nc.gpsimd.memset(eps[:], EPS)
+        all_s = held.tile([T, P], F32, name="all_s")
+        nc.gpsimd.memset(all_s[:], float(S))
+        identity = held.tile([T, T], F32, name="identity")
+        make_identity(nc, identity[:])
+
+        top = held.tile([P, T], F32, name="top")
+        shifted = held.tile([P, N], F32, name="shifted")
+
+        def weight_step(w):
+            return slice(w * W_PIECE, (w + 1) * W_PIECE), slice(w * W_TEAMS, (w + 1) * W_TEAMS)
+
+        for k in range(PIECES):
+            steps_of_piece = range(k * PIECE // W_PIECE, (k + 1) * PIECE // W_PIECE)
+            for w in steps_of_piece:
+                entries, teams = weight_step(w)
+                nc.vector.tensor_reduce(
+                    out=top[:, teams], in_=scores[:, entries].rearrange(BY_TEAM, l=L),
+                    axis=AXIS.X, op=ALU.max,
+                )
+            for w in steps_of_piece:
+                entries, teams = weight_step(w)
+                nc.vector.tensor_tensor(
+                    out=shifted[:, entries].rearrange(BY_TEAM, l=L),
+                    in0=scores[:, entries].rearrange(BY_TEAM, l=L),
+                    in1=top[:, teams].unsqueeze(2).to_broadcast([P, W_TEAMS, L]),
+                    op=ALU.subtract,
+                )
+
+        relu = [held.tile([P, S], F32, name=f"relu{b}") for b in range(BLOCKS)]
+        means = held.tile([P, BLOCKS], F32, name="means")
+        expd = held.tile([P, N], F32, name="expd")
+        def exp_piece(k):
+            for w in range(k * PIECE // W_PIECE, (k + 1) * PIECE // W_PIECE):
+                entries, teams = weight_step(w)
+                nc.scalar.activation(out=expd[:, entries], in_=shifted[:, entries], func=ACT.Exp)
+
+        def relu_block(b):
+            nc.scalar.activation(
+                out=relu[b][:], in_=raw[b][:], func=ACT.Relu, scale=1.0 / S,
+                accum_out=means[:, b : b + 1],
+            )
+
+        relu_block(0)
+        exp_piece(0)
+        relu_block(1)
+
+        team_minus_top = held.tile([T, 1], F32, name="team_minus_top")
+        nc.vector.tensor_reduce(
+            out=team_minus_top[:], in_=team_scores[:], axis=AXIS.X, op=ALU.max, negate=True
+        )
+        team_expd = held.tile([T, L], F32, name="team_expd")
+        team_den = held.tile([T, 1], F32, name="team_den")
+        nc.scalar.activation(
+            out=team_expd[:], in_=team_scores[:], func=ACT.Exp,
+            bias=team_minus_top[:], accum_out=team_den[:],
+        )
+
+        team_rden = held.tile([T, 1], F32, name="team_rden")
+        nc.vector.reciprocal(out=team_rden[:], in_=team_den[:])
+        diagonal = held.tile([T, T], F32, name="diagonal")
+        nc.scalar.activation(out=diagonal[:], in_=identity[:], func=ACT.Copy, scale=team_rden[:])
+        rden = psum.tile([P, T], F32, name="rden")
+        nc.tensor.matmul(rden[:], all_s[:], diagonal[:], start=True, stop=True)
+
+        exp_piece(1)
+
+        squares = held.tile([P, BLOCKS], F32, name="squares")
+        for b in range(BLOCKS):
+            centred_sq = held.tile([P, S], F32, name=f"centred_sq{b}")
+            nc.scalar.activation(
+                out=centred_sq[:], in_=relu[b][:], func=ACT.Square,
+                scale=-float(S), bias=means[:, b : b + 1], accum_out=squares[:, b : b + 1],
+            )
+        rstd = held.tile([P, BLOCKS], F32, name="rstd")
+        minus_mean_gain = held.tile([P, BLOCKS], F32, name="minus_mean_gain")
+        var_eps = held.tile([P, BLOCKS], F32, name="var_eps")
+        nc.scalar.activation(
+            out=var_eps[:], in_=squares[:], func=ACT.Identity, scale=1.0 / S, bias=eps[:]
+        )
+        nc.gpsimd.tensor_tensor(out=rstd[:], in0=var_eps[:], in1=minus_half[:], op=ALU.pow)
+        for b in range(BLOCKS):
+            block = slice(b, b + 1)
+            nc.scalar.activation(
+                out=minus_mean_gain[:, block], in_=means[:, block], func=ACT.Copy,
+                scale=minus_gains[:, block],
+            )
+        shift = held.tile([P, BLOCKS], F32, name="shift")
+        for b in range(BLOCKS):
+            block = slice(b, b + 1)
+            nc.scalar.activation(
+                out=shift[:, block], in_=rstd[:, block], func=ACT.Identity,
+                scale=minus_mean_gain[:, block], bias=betas[:, block],
+            )
+
+        picked = held.tile([P, BLOCKS, N], F32, name="picked")
+        summed = held.tile([P, BLOCKS, T], F32, name="summed")
+
+        def sum_teams(b, k):
+            nc.vector.tensor_reduce(
+                out=summed[:, b, k * PIECE_TEAMS : (k + 1) * PIECE_TEAMS],
+                in_=picked[:, b, k * PIECE : (k + 1) * PIECE].rearrange(BY_TEAM, l=L),
+                axis=AXIS.X, op=ALU.add,
+            )
+
+        steps = [(b, k) for b in range(BLOCKS) for k in range(PIECES)]
+        for i, (b, k) in enumerate(steps):
+            nc.vector.tensor_tensor(
+                out=picked[:, b, k * PIECE : (k + 1) * PIECE],
+                in0=relu[b][:].indirect(offsets[:, k * PIECE // 16 : (k + 1) * PIECE // 16]),
+                in1=expd[:, k * PIECE : (k + 1) * PIECE],
+                op=ALU.mult,
+            )
+            if i > 0:
+                sum_teams(*steps[i - 1])
+        sum_teams(*steps[-1])
+
+        normed = held.tile([P, BLOCKS, T], F32, name="normed")
+        result = held.tile([P, BLOCKS, T], F32, name="result")
+        for b in range(BLOCKS):
+            nc.vector.scalar_tensor_tensor(
+                out=normed[:, b, :], in0=summed[:, b, :], scalar=rstd[:, b : b + 1], in1=rden[:],
+                op0=ALU.mult, op1=ALU.mult,
+            )
+        for b in range(BLOCKS):
+            nc.vector.tensor_scalar(
+                out=result[:, b, :], in0=normed[:, b, :],
+                scalar1=gains[:, b : b + 1], scalar2=shift[:, b : b + 1],
+                op0=ALU.mult, op1=ALU.add,
+            )
+        nc.sync.dma_start(out.rearrange("(p b) t -> p b t", b=BLOCKS), result[:])

@@ -14,8 +14,10 @@ BLOCKS = C // P
 PIECE = S
 PIECES = N // PIECE
 PIECE_TEAMS = PIECE // L
-W_PIECE = 128
-W_TEAMS = W_PIECE // L
+SQ = 32
+ROWS = N // SQ
+ROW_TEAMS = SQ // L
+PIECE_ROWS = PIECE // SQ
 BY_TEAM = "p (t l) -> p t l"
 
 
@@ -26,63 +28,75 @@ def tile_tag_kernel(tc, h, gain, beta, att, offs, out):
         tc.psum_pool(name="psum", bufs=1) as psum,
     ):
         offsets = held.tile([P, N // 16], U16, name="offsets")
-        scores = held.tile([P, N], F32, name="scores")
-        nc.sync.dma_start(scores[:], att.broadcast_to([P, N]))
+        scores = held.tile([P, SQ], F32, name="scores")
+        nc.gpsimd.memset(scores[:], 0.0)
+        rows = att.rearrange("o (c f) -> (o c) f", f=SQ)
+        for g in range(P // SQ):
+            nc.sync.dma_start(scores[g * SQ : g * SQ + ROWS, :], rows)
         raw = [held.tile([P, S], F32, name=f"raw{b}") for b in range(BLOCKS)]
         for b in range(BLOCKS):
             nc.sync.dma_start(raw[b][:], h.rearrange("(p b) s -> b p s", b=BLOCKS)[b])
         nc.sync.dma_start(offsets[:], offs)
-        team_scores = held.tile([T, L], F32, name="team_scores")
-        nc.sync.dma_start(team_scores[:], att.rearrange("o (t l) -> (o t) l", l=L))
         gains = held.tile([P, BLOCKS], F32, name="gains")
         betas = held.tile([P, BLOCKS], F32, name="betas")
         nc.sync.dma_start(gains[:], gain.rearrange("(p b) o -> p (b o)", b=BLOCKS))
         nc.sync.dma_start(betas[:], beta.rearrange("(p b) o -> p (b o)", b=BLOCKS))
 
-        minus_gains = held.tile([P, BLOCKS], F32, name="minus_gains")
-        nc.gpsimd.tensor_scalar(
-            out=minus_gains[:], in0=gains[:], scalar1=-1.0, scalar2=None, op0=ALU.mult
-        )
-
         minus_half = held.tile([P, BLOCKS], F32, name="minus_half")
         nc.gpsimd.memset(minus_half[:], -0.5)
+        minus_one = held.tile([SQ, ROW_TEAMS], F32, name="minus_one")
+        nc.gpsimd.memset(minus_one[:], -1.0)
         eps = held.tile([P, 1], F32, name="eps")
         nc.gpsimd.memset(eps[:], EPS)
-        all_s = held.tile([T, P], F32, name="all_s")
+        all_s = held.tile([SQ, P], F32, name="all_s")
         nc.gpsimd.memset(all_s[:], float(S))
-        identity = held.tile([T, T], F32, name="identity")
+        identity = held.tile([SQ, SQ], F32, name="identity")
         make_identity(nc, identity[:])
 
-        top = held.tile([P, T], F32, name="top")
-        shifted = held.tile([P, N], F32, name="shifted")
+        top = held.tile([P, ROW_TEAMS], F32, name="top")
+        nc.vector.tensor_reduce(
+            out=top[:], in_=scores[:].rearrange(BY_TEAM, l=L), axis=AXIS.X, op=ALU.max
+        )
+        shifted = held.tile([P, SQ], F32, name="shifted", align_bytes=64)
+        nc.vector.tensor_tensor(
+            out=shifted[:].rearrange(BY_TEAM, l=L), in0=scores[:].rearrange(BY_TEAM, l=L),
+            in1=top[:].unsqueeze(2).to_broadcast([P, ROW_TEAMS, L]), op=ALU.subtract,
+        )
+        columns = held.tile([P, SQ], F32, name="columns", align_bytes=64)
+        nc.vector.transpose(columns[:], shifted[:])
 
-        def weight_step(w):
-            return slice(w * W_PIECE, (w + 1) * W_PIECE), slice(w * W_TEAMS, (w + 1) * W_TEAMS)
-
-        for k in range(PIECES):
-            steps_of_piece = range(k * PIECE // W_PIECE, (k + 1) * PIECE // W_PIECE)
-            for w in steps_of_piece:
-                entries, teams = weight_step(w)
-                nc.vector.tensor_reduce(
-                    out=top[:, teams], in_=scores[:, entries].rearrange(BY_TEAM, l=L),
-                    axis=AXIS.X, op=ALU.max,
-                )
-            for w in steps_of_piece:
-                entries, teams = weight_step(w)
-                nc.vector.tensor_tensor(
-                    out=shifted[:, entries].rearrange(BY_TEAM, l=L),
-                    in0=scores[:, entries].rearrange(BY_TEAM, l=L),
-                    in1=top[:, teams].unsqueeze(2).to_broadcast([P, W_TEAMS, L]),
-                    op=ALU.subtract,
-                )
+        row_expd = held.tile([SQ, SQ], F32, name="row_expd")
+        row_den = held.tile([SQ, ROW_TEAMS], F32, name="row_den")
+        for d in range(ROW_TEAMS):
+            team = slice(d * L, (d + 1) * L)
+            nc.scalar.activation(
+                out=row_expd[:, team], in_=shifted[0:SQ, team], func=ACT.Exp,
+                accum_out=row_den[:, d : d + 1],
+            )
+        row_rden = held.tile([SQ, ROW_TEAMS], F32, name="row_rden")
+        nc.gpsimd.tensor_tensor(out=row_rden[:], in0=row_den[:], in1=minus_one[:], op=ALU.pow)
+        diagonal = held.tile([SQ, T], F32, name="diagonal")
+        nc.gpsimd.tensor_tensor(
+            out=diagonal[:].rearrange("p (c d) -> p c d", d=ROW_TEAMS),
+            in0=identity[:, 0:ROWS].unsqueeze(2).to_broadcast([SQ, ROWS, ROW_TEAMS]),
+            in1=row_rden[:].unsqueeze(1).to_broadcast([SQ, ROWS, ROW_TEAMS]), op=ALU.mult,
+        )
+        rden = psum.tile([P, T], F32, name="rden")
+        nc.tensor.matmul(rden[:], all_s[:], diagonal[:], start=True, stop=True)
 
         relu = [held.tile([P, S], F32, name=f"relu{b}") for b in range(BLOCKS)]
         means = held.tile([P, BLOCKS], F32, name="means")
-        expd = held.tile([P, N], F32, name="expd")
+        repeated = [held.tile([P, PIECE], F32, name=f"repeated{k}", align_bytes=64) for k in range(PIECES)]
+        expd = [held.tile([P, PIECE], F32, name=f"expd{k}", align_bytes=64) for k in range(PIECES)]
+
         def exp_piece(k):
-            for w in range(k * PIECE // W_PIECE, (k + 1) * PIECE // W_PIECE):
-                entries, teams = weight_step(w)
-                nc.scalar.activation(out=expd[:, entries], in_=shifted[:, entries], func=ACT.Exp)
+            nc.scalar.activation(
+                out=repeated[k][:].rearrange("p (c f) -> p c f", f=SQ),
+                in_=columns[:, k * PIECE_ROWS : (k + 1) * PIECE_ROWS]
+                .unsqueeze(2).to_broadcast([P, PIECE_ROWS, SQ]),
+                func=ACT.Exp,
+            )
+            nc.vector.transpose(expd[k][:], repeated[k][:])
 
         def relu_block(b):
             nc.scalar.activation(
@@ -90,29 +104,10 @@ def tile_tag_kernel(tc, h, gain, beta, att, offs, out):
                 accum_out=means[:, b : b + 1],
             )
 
-        relu_block(0)
         exp_piece(0)
-        relu_block(1)
-
-        team_minus_top = held.tile([T, 1], F32, name="team_minus_top")
-        nc.vector.tensor_reduce(
-            out=team_minus_top[:], in_=team_scores[:], axis=AXIS.X, op=ALU.max, negate=True
-        )
-        team_expd = held.tile([T, L], F32, name="team_expd")
-        team_den = held.tile([T, 1], F32, name="team_den")
-        nc.scalar.activation(
-            out=team_expd[:], in_=team_scores[:], func=ACT.Exp,
-            bias=team_minus_top[:], accum_out=team_den[:],
-        )
-
-        team_rden = held.tile([T, 1], F32, name="team_rden")
-        nc.vector.reciprocal(out=team_rden[:], in_=team_den[:])
-        diagonal = held.tile([T, T], F32, name="diagonal")
-        nc.scalar.activation(out=diagonal[:], in_=identity[:], func=ACT.Copy, scale=team_rden[:])
-        rden = psum.tile([P, T], F32, name="rden")
-        nc.tensor.matmul(rden[:], all_s[:], diagonal[:], start=True, stop=True)
-
+        relu_block(0)
         exp_piece(1)
+        relu_block(1)
 
         squares = held.tile([P, BLOCKS], F32, name="squares")
         for b in range(BLOCKS):
@@ -121,18 +116,20 @@ def tile_tag_kernel(tc, h, gain, beta, att, offs, out):
                 out=centred_sq[:], in_=relu[b][:], func=ACT.Square,
                 scale=-float(S), bias=means[:, b : b + 1], accum_out=squares[:, b : b + 1],
             )
-        rstd = held.tile([P, BLOCKS], F32, name="rstd")
-        minus_mean_gain = held.tile([P, BLOCKS], F32, name="minus_mean_gain")
         var_eps = held.tile([P, BLOCKS], F32, name="var_eps")
         nc.scalar.activation(
             out=var_eps[:], in_=squares[:], func=ACT.Identity, scale=1.0 / S, bias=eps[:]
         )
+        rstd = held.tile([P, BLOCKS], F32, name="rstd")
         nc.gpsimd.tensor_tensor(out=rstd[:], in0=var_eps[:], in1=minus_half[:], op=ALU.pow)
+        minus_means = held.tile([P, BLOCKS], F32, name="minus_means")
+        nc.scalar.activation(out=minus_means[:], in_=means[:], func=ACT.Copy, scale=-1.0)
+        minus_mean_gain = held.tile([P, BLOCKS], F32, name="minus_mean_gain")
         for b in range(BLOCKS):
             block = slice(b, b + 1)
             nc.scalar.activation(
-                out=minus_mean_gain[:, block], in_=means[:, block], func=ACT.Copy,
-                scale=minus_gains[:, block],
+                out=minus_mean_gain[:, block], in_=minus_means[:, block], func=ACT.Copy,
+                scale=gains[:, block],
             )
         shift = held.tile([P, BLOCKS], F32, name="shift")
         for b in range(BLOCKS):
@@ -157,7 +154,7 @@ def tile_tag_kernel(tc, h, gain, beta, att, offs, out):
             nc.vector.tensor_tensor(
                 out=picked[:, b, k * PIECE : (k + 1) * PIECE],
                 in0=relu[b][:].indirect(offsets[:, k * PIECE // 16 : (k + 1) * PIECE // 16]),
-                in1=expd[:, k * PIECE : (k + 1) * PIECE],
+                in1=expd[k][:],
                 op=ALU.mult,
             )
             if i > 0:

@@ -1,5 +1,4 @@
 import concourse.mybir as mybir
-from concourse.masks import make_identity
 
 F32 = mybir.dt.float32
 U16 = mybir.dt.uint16
@@ -15,10 +14,12 @@ PIECE = S
 PIECES = N // PIECE
 PIECE_TEAMS = PIECE // L
 SQ = 32
+GROUPS = P // SQ
 ROWS = N // SQ
 ROW_TEAMS = SQ // L
 PIECE_ROWS = PIECE // SQ
 BY_TEAM = "p (t l) -> p t l"
+BY_ROW = "p (c d) -> p c d"
 
 
 def tile_tag_kernel(tc, h, gain, beta, att, offs, out):
@@ -28,11 +29,8 @@ def tile_tag_kernel(tc, h, gain, beta, att, offs, out):
         tc.psum_pool(name="psum", bufs=1) as psum,
     ):
         offsets = held.tile([P, N // 16], U16, name="offsets")
-        scores = held.tile([P, SQ], F32, name="scores")
-        nc.gpsimd.memset(scores[:], 0.0)
-        rows = att.rearrange("o (c f) -> (o c) f", f=SQ)
-        for g in range(P // SQ):
-            nc.sync.dma_start(scores[g * SQ : g * SQ + ROWS, :], rows)
+        scores = held.tile([T, L], F32, name="scores")
+        nc.sync.dma_start(scores[:], att.rearrange("o (t l) -> (o t) l", l=L))
         raw = [held.tile([P, S], F32, name=f"raw{b}") for b in range(BLOCKS)]
         for b in range(BLOCKS):
             nc.sync.dma_start(raw[b][:], h.rearrange("(p b) s -> b p s", b=BLOCKS)[b])
@@ -42,61 +40,95 @@ def tile_tag_kernel(tc, h, gain, beta, att, offs, out):
         nc.sync.dma_start(gains[:], gain.rearrange("(p b) o -> p (b o)", b=BLOCKS))
         nc.sync.dma_start(betas[:], beta.rearrange("(p b) o -> p (b o)", b=BLOCKS))
 
-        minus_half = held.tile([P, BLOCKS], F32, name="minus_half")
-        nc.gpsimd.memset(minus_half[:], -0.5)
-        minus_one = held.tile([SQ, ROW_TEAMS], F32, name="minus_one")
-        nc.gpsimd.memset(minus_one[:], -1.0)
         eps = held.tile([P, 1], F32, name="eps")
         nc.gpsimd.memset(eps[:], EPS)
-        all_s = held.tile([SQ, P], F32, name="all_s")
+        all_s = held.tile([T, P], F32, name="all_s")
         nc.gpsimd.memset(all_s[:], float(S))
-        identity = held.tile([SQ, SQ], F32, name="identity")
-        make_identity(nc, identity[:])
-
-        top = held.tile([P, ROW_TEAMS], F32, name="top")
+        minus_half = held.tile([P, BLOCKS], F32, name="minus_half")
+        nc.gpsimd.memset(minus_half[:], -0.5)
+        warm = held.tile([P, 1], F32, name="warm")
+        nc.scalar.activation(out=warm[:], in_=eps[:], func=ACT.Exp)
+        ones = held.tile([P, SQ], F32, name="ones")
+        nc.vector.memset(ones[:], 1.0)
+        column = held.tile([P, SQ], F32, name="column", align_bytes=64)
+        nc.vector.tensor_tensor_scan(
+            column[:], ones[:], ones[:], -1.0, op0=ALU.mult, op1=ALU.add
+        )
+        partition = held.tile([P, SQ], F32, name="partition", align_bytes=64)
+        nc.vector.transpose(partition[:], column[:])
+        identity = held.tile([T, T], F32, name="identity")
+        nc.vector.tensor_scalar(
+            out=identity[:], in0=column[0:T, :], scalar1=partition[0:T, 0:1], scalar2=None,
+            op0=ALU.is_equal,
+        )
+        row_of_team = held.tile([T, ROWS], F32, name="row_of_team")
         nc.vector.tensor_reduce(
-            out=top[:], in_=scores[:].rearrange(BY_TEAM, l=L), axis=AXIS.X, op=ALU.max
+            out=row_of_team[:], in_=identity[:].rearrange(BY_ROW, d=ROW_TEAMS),
+            axis=AXIS.X, op=ALU.max,
         )
-        shifted = held.tile([P, SQ], F32, name="shifted", align_bytes=64)
-        nc.vector.tensor_tensor(
-            out=shifted[:].rearrange(BY_TEAM, l=L), in0=scores[:].rearrange(BY_TEAM, l=L),
-            in1=top[:].unsqueeze(2).to_broadcast([P, ROW_TEAMS, L]), op=ALU.subtract,
+        place_of_team = held.tile([T, ROW_TEAMS], F32, name="place_of_team")
+        nc.vector.tensor_reduce(
+            out=place_of_team[:], in_=identity[:].rearrange("p (c d) -> p d c", d=ROW_TEAMS),
+            axis=AXIS.X, op=ALU.max,
         )
-        columns = held.tile([P, SQ], F32, name="columns", align_bytes=64)
-        nc.vector.transpose(columns[:], shifted[:])
 
-        row_expd = held.tile([SQ, SQ], F32, name="row_expd")
-        row_den = held.tile([SQ, ROW_TEAMS], F32, name="row_den")
-        for d in range(ROW_TEAMS):
-            team = slice(d * L, (d + 1) * L)
-            nc.scalar.activation(
-                out=row_expd[:, team], in_=shifted[0:SQ, team], func=ACT.Exp,
-                accum_out=row_den[:, d : d + 1],
-            )
-        row_rden = held.tile([SQ, ROW_TEAMS], F32, name="row_rden")
-        nc.gpsimd.tensor_tensor(out=row_rden[:], in0=row_den[:], in1=minus_one[:], op=ALU.pow)
-        diagonal = held.tile([SQ, T], F32, name="diagonal")
-        nc.gpsimd.tensor_tensor(
-            out=diagonal[:].rearrange("p (c d) -> p c d", d=ROW_TEAMS),
-            in0=identity[:, 0:ROWS].unsqueeze(2).to_broadcast([SQ, ROWS, ROW_TEAMS]),
-            in1=row_rden[:].unsqueeze(1).to_broadcast([SQ, ROWS, ROW_TEAMS]), op=ALU.mult,
+        minus_top = held.tile([T, 1], F32, name="minus_top")
+        nc.vector.tensor_reduce(
+            out=minus_top[:], in_=scores[:], axis=AXIS.X, op=ALU.max, negate=True
         )
-        rden = psum.tile([P, T], F32, name="rden")
+        def place(name, values, op, scalar):
+            placed = held.tile([T, P], F32, name=name)
+            for d in range(ROW_TEAMS):
+                nc.vector.tensor_scalar(
+                    out=placed[:].rearrange("p (g d l) -> p g d l", d=ROW_TEAMS, l=L)[:, :, d, :],
+                    in0=values[:].unsqueeze(1).to_broadcast([T, GROUPS, L]),
+                    scalar1=scalar[:], scalar2=place_of_team[:, d : d + 1],
+                    op0=op, op1=ALU.mult,
+                )
+            return placed
+
+        def columns_of(k, placed):
+            columns = psum.tile([P, PIECE_ROWS], F32, name=f"columns{k}")
+            nc.tensor.matmul(
+                columns[:], placed[:], row_of_team[:, k * PIECE_ROWS : (k + 1) * PIECE_ROWS],
+                start=True, stop=True,
+            )
+            return columns
+
+        columns0 = columns_of(0, place("placed0", scores, ALU.add, minus_top))
+
+        team_expd = held.tile([T, L], F32, name="team_expd")
+        team_den = held.tile([T, 1], F32, name="team_den")
+        nc.scalar.activation(
+            out=team_expd[:], in_=scores[:], func=ACT.Exp,
+            bias=minus_top[:], accum_out=team_den[:],
+        )
+        team_rden = held.tile([T, 1], F32, name="team_rden")
+        nc.vector.reciprocal(out=team_rden[:], in_=team_den[:])
+        columns1 = columns_of(1, place("placed1", team_expd, ALU.mult, team_rden))
+        diagonal = held.tile([T, PIECE_TEAMS], F32, name="diagonal")
+        nc.vector.tensor_scalar(
+            out=diagonal[:], in0=identity[:, 0:PIECE_TEAMS], scalar1=team_rden[:], scalar2=None,
+            op0=ALU.mult,
+        )
+        rden = psum.tile([P, PIECE_TEAMS], F32, name="rden")
         nc.tensor.matmul(rden[:], all_s[:], diagonal[:], start=True, stop=True)
 
         relu = [held.tile([P, S], F32, name=f"relu{b}") for b in range(BLOCKS)]
         means = held.tile([P, BLOCKS], F32, name="means")
-        repeated = [held.tile([P, PIECE], F32, name=f"repeated{k}", align_bytes=64) for k in range(PIECES)]
-        expd = [held.tile([P, PIECE], F32, name=f"expd{k}", align_bytes=64) for k in range(PIECES)]
+        weights = [held.tile([P, PIECE], F32, name=f"weights{k}", align_bytes=64) for k in range(PIECES)]
 
-        def exp_piece(k):
-            nc.scalar.activation(
-                out=repeated[k][:].rearrange("p (c f) -> p c f", f=SQ),
-                in_=columns[:, k * PIECE_ROWS : (k + 1) * PIECE_ROWS]
-                .unsqueeze(2).to_broadcast([P, PIECE_ROWS, SQ]),
-                func=ACT.Exp,
-            )
-            nc.vector.transpose(expd[k][:], repeated[k][:])
+        def spread(k, columns, step, func, scale):
+            repeated = held.tile([P, PIECE], F32, name=f"repeated{k}", align_bytes=64)
+            for first in range(0, PIECE, step):
+                entries = slice(first, first + step)
+                nc.scalar.activation(
+                    out=repeated[:, entries].rearrange("p (c f) -> p c f", f=SQ),
+                    in_=columns[:, first // SQ : (first + step) // SQ]
+                    .unsqueeze(2).to_broadcast([P, step // SQ, SQ]),
+                    func=func, scale=scale,
+                )
+                nc.vector.transpose(weights[k][:, entries], repeated[:, entries])
 
         def relu_block(b):
             nc.scalar.activation(
@@ -104,10 +136,10 @@ def tile_tag_kernel(tc, h, gain, beta, att, offs, out):
                 accum_out=means[:, b : b + 1],
             )
 
-        exp_piece(0)
         relu_block(0)
-        exp_piece(1)
+        spread(0, columns0, PIECE // 2, ACT.Exp, 1.0)
         relu_block(1)
+        spread(1, columns1, PIECE, ACT.Copy, float(S))
 
         squares = held.tile([P, BLOCKS], F32, name="squares")
         for b in range(BLOCKS):
@@ -131,47 +163,54 @@ def tile_tag_kernel(tc, h, gain, beta, att, offs, out):
                 out=minus_mean_gain[:, block], in_=minus_means[:, block], func=ACT.Copy,
                 scale=gains[:, block],
             )
+        scale = held.tile([P, BLOCKS], F32, name="scale")
         shift = held.tile([P, BLOCKS], F32, name="shift")
         for b in range(BLOCKS):
             block = slice(b, b + 1)
+            nc.scalar.activation(
+                out=scale[:, block], in_=rstd[:, block], func=ACT.Copy, scale=gains[:, block]
+            )
             nc.scalar.activation(
                 out=shift[:, block], in_=rstd[:, block], func=ACT.Identity,
                 scale=minus_mean_gain[:, block], bias=betas[:, block],
             )
 
-        picked = held.tile([P, BLOCKS, N], F32, name="picked")
-        summed = held.tile([P, BLOCKS, T], F32, name="summed")
+        picked = held.tile([P, N // PIECE, BLOCKS, PIECE], F32, name="picked")
+        unscaled = held.tile([P, BLOCKS, PIECE_TEAMS], F32, name="unscaled")
+        pooled = held.tile([P, BLOCKS, T], F32, name="pooled")
 
-        def sum_teams(b, k):
-            nc.vector.tensor_reduce(
-                out=summed[:, b, k * PIECE_TEAMS : (k + 1) * PIECE_TEAMS],
-                in_=picked[:, b, k * PIECE : (k + 1) * PIECE].rearrange(BY_TEAM, l=L),
-                axis=AXIS.X, op=ALU.add,
-            )
-
-        steps = [(b, k) for b in range(BLOCKS) for k in range(PIECES)]
-        for i, (b, k) in enumerate(steps):
+        def look_up(k, b):
             nc.vector.tensor_tensor(
-                out=picked[:, b, k * PIECE : (k + 1) * PIECE],
+                out=picked[:, k, b, :],
                 in0=relu[b][:].indirect(offsets[:, k * PIECE // 16 : (k + 1) * PIECE // 16]),
-                in1=expd[k][:],
+                in1=weights[k][:],
                 op=ALU.mult,
             )
-            if i > 0:
-                sum_teams(*steps[i - 1])
-        sum_teams(*steps[-1])
 
-        normed = held.tile([P, BLOCKS, T], F32, name="normed")
+        def sum_teams(k, b):
+            sums = unscaled[:, b, :] if k == 0 else pooled[:, b, PIECE_TEAMS:]
+            nc.vector.tensor_reduce(
+                out=sums, in_=picked[:, k, b, :].rearrange(BY_TEAM, l=L), axis=AXIS.X, op=ALU.add
+            )
+
+        look_up(0, 0)
+        look_up(0, 1)
+        sum_teams(0, 0)
+        look_up(1, 0)
+        sum_teams(0, 1)
+        look_up(1, 1)
+        sum_teams(1, 0)
+        nc.vector.tensor_tensor(
+            out=pooled[:, :, 0:PIECE_TEAMS], in0=unscaled[:],
+            in1=rden[:].unsqueeze(1).to_broadcast([P, BLOCKS, PIECE_TEAMS]), op=ALU.mult,
+        )
+        sum_teams(1, 1)
+
         result = held.tile([P, BLOCKS, T], F32, name="result")
         for b in range(BLOCKS):
-            nc.vector.scalar_tensor_tensor(
-                out=normed[:, b, :], in0=summed[:, b, :], scalar=rstd[:, b : b + 1], in1=rden[:],
-                op0=ALU.mult, op1=ALU.mult,
-            )
-        for b in range(BLOCKS):
             nc.vector.tensor_scalar(
-                out=result[:, b, :], in0=normed[:, b, :],
-                scalar1=gains[:, b : b + 1], scalar2=shift[:, b : b + 1],
+                out=result[:, b, :], in0=pooled[:, b, :],
+                scalar1=scale[:, b : b + 1], scalar2=shift[:, b : b + 1],
                 op0=ALU.mult, op1=ALU.add,
             )
         nc.sync.dma_start(out.rearrange("(p b) t -> p b t", b=BLOCKS), result[:])

@@ -13,13 +13,9 @@ BLOCKS = C // P
 PIECE = S
 PIECES = N // PIECE
 PIECE_TEAMS = PIECE // L
-SQ = 32
-GROUPS = P // SQ
-ROWS = N // SQ
-ROW_TEAMS = SQ // L
-PIECE_ROWS = PIECE // SQ
+STEP = PIECE // 2
+STEPS = PIECE // STEP
 BY_TEAM = "p (t l) -> p t l"
-BY_ROW = "p (c d) -> p c d"
 
 
 def tile_tag_kernel(tc, h, gain, beta, att, offs, out):
@@ -31,9 +27,8 @@ def tile_tag_kernel(tc, h, gain, beta, att, offs, out):
         offsets = held.tile([P, N // 16], U16, name="offsets")
         scores = held.tile([T, L], F32, name="scores")
         nc.sync.dma_start(scores[:], att.rearrange("o (t l) -> (o t) l", l=L))
-        raw = [held.tile([P, S], F32, name=f"raw{b}") for b in range(BLOCKS)]
-        for b in range(BLOCKS):
-            nc.sync.dma_start(raw[b][:], h.rearrange("(p b) s -> b p s", b=BLOCKS)[b])
+        raw = held.tile([P, BLOCKS, S], F32, name="raw")
+        nc.sync.dma_start(raw[:], h.rearrange("(p b) s -> p b s", b=BLOCKS))
         nc.sync.dma_start(offsets[:], offs)
         gains = held.tile([P, BLOCKS], F32, name="gains")
         betas = held.tile([P, BLOCKS], F32, name="betas")
@@ -42,60 +37,48 @@ def tile_tag_kernel(tc, h, gain, beta, att, offs, out):
 
         eps = held.tile([P, 1], F32, name="eps")
         nc.gpsimd.memset(eps[:], EPS)
-        all_s = held.tile([T, P], F32, name="all_s")
-        nc.gpsimd.memset(all_s[:], float(S))
+        all_ones = held.tile([T, P], F32, name="all_ones")
+        nc.gpsimd.memset(all_ones[:], 1.0)
         minus_half = held.tile([P, BLOCKS], F32, name="minus_half")
         nc.gpsimd.memset(minus_half[:], -0.5)
         warm = held.tile([P, 1], F32, name="warm")
         nc.scalar.activation(out=warm[:], in_=eps[:], func=ACT.Exp)
-        ones = held.tile([P, SQ], F32, name="ones")
+        ones = held.tile([P, T], F32, name="ones")
         nc.vector.memset(ones[:], 1.0)
-        column = held.tile([P, SQ], F32, name="column", align_bytes=64)
+        column = held.tile([P, T], F32, name="column", align_bytes=64)
         nc.vector.tensor_tensor_scan(
             column[:], ones[:], ones[:], -1.0, op0=ALU.mult, op1=ALU.add
         )
-        partition = held.tile([P, SQ], F32, name="partition", align_bytes=64)
+        partition = held.tile([P, T], F32, name="partition", align_bytes=64)
         nc.vector.transpose(partition[:], column[:])
         identity = held.tile([T, T], F32, name="identity")
         nc.vector.tensor_scalar(
             out=identity[:], in0=column[0:T, :], scalar1=partition[0:T, 0:1], scalar2=None,
             op0=ALU.is_equal,
         )
-        row_of_team = held.tile([T, ROWS], F32, name="row_of_team")
-        nc.vector.tensor_reduce(
-            out=row_of_team[:], in_=identity[:].rearrange(BY_ROW, d=ROW_TEAMS),
-            axis=AXIS.X, op=ALU.max,
-        )
-        place_of_team = held.tile([T, ROW_TEAMS], F32, name="place_of_team")
-        nc.vector.tensor_reduce(
-            out=place_of_team[:], in_=identity[:].rearrange("p (c d) -> p d c", d=ROW_TEAMS),
-            axis=AXIS.X, op=ALU.max,
-        )
 
         minus_top = held.tile([T, 1], F32, name="minus_top")
         nc.vector.tensor_reduce(
             out=minus_top[:], in_=scores[:], axis=AXIS.X, op=ALU.max, negate=True
         )
-        def place(name, values, op, scalar):
-            placed = held.tile([T, P], F32, name=name)
-            for d in range(ROW_TEAMS):
-                nc.vector.tensor_scalar(
-                    out=placed[:].rearrange("p (g d l) -> p g d l", d=ROW_TEAMS, l=L)[:, :, d, :],
-                    in0=values[:].unsqueeze(1).to_broadcast([T, GROUPS, L]),
-                    scalar1=scalar[:], scalar2=place_of_team[:, d : d + 1],
-                    op0=op, op1=ALU.mult,
-                )
-            return placed
 
-        def columns_of(k, placed):
-            columns = psum.tile([P, PIECE_ROWS], F32, name=f"columns{k}")
-            nc.tensor.matmul(
-                columns[:], placed[:], row_of_team[:, k * PIECE_ROWS : (k + 1) * PIECE_ROWS],
-                start=True, stop=True,
+        def row_of(name, values, op, scalar, first, entries):
+            teams = slice(first // L, (first + entries) // L)
+            shape = [T, entries // L, L]
+            placed = held.tile([T, entries], F32, name=f"placed_{name}")
+            nc.vector.scalar_tensor_tensor(
+                out=placed[:].rearrange(BY_TEAM, l=L),
+                in0=values[:].unsqueeze(1).to_broadcast(shape), scalar=scalar[:],
+                in1=identity[:, teams].unsqueeze(2).to_broadcast(shape),
+                op0=op, op1=ALU.mult,
             )
-            return columns
+            row = psum.tile([P, entries], F32, name=f"row_{name}")
+            nc.tensor.matmul(row[:], all_ones[:], placed[:], start=True, stop=True)
+            return row
 
-        columns0 = columns_of(0, place("placed0", scores, ALU.add, minus_top))
+        shifted = [
+            row_of(f"shifted{w}", scores, ALU.add, minus_top, w * STEP, STEP) for w in range(STEPS)
+        ]
 
         team_expd = held.tile([T, L], F32, name="team_expd")
         team_den = held.tile([T, 1], F32, name="team_den")
@@ -105,41 +88,31 @@ def tile_tag_kernel(tc, h, gain, beta, att, offs, out):
         )
         team_rden = held.tile([T, 1], F32, name="team_rden")
         nc.vector.reciprocal(out=team_rden[:], in_=team_den[:])
-        columns1 = columns_of(1, place("placed1", team_expd, ALU.mult, team_rden))
+        weights_row = row_of("weights", team_expd, ALU.mult, team_rden, PIECE, PIECE)
         diagonal = held.tile([T, PIECE_TEAMS], F32, name="diagonal")
         nc.vector.tensor_scalar(
-            out=diagonal[:], in0=identity[:, 0:PIECE_TEAMS], scalar1=team_rden[:], scalar2=None,
-            op0=ALU.mult,
+            out=diagonal[:], in0=identity[:, 0:PIECE_TEAMS], scalar1=team_rden[:],
+            scalar2=float(S), op0=ALU.mult, op1=ALU.mult,
         )
         rden = psum.tile([P, PIECE_TEAMS], F32, name="rden")
-        nc.tensor.matmul(rden[:], all_s[:], diagonal[:], start=True, stop=True)
+        nc.tensor.matmul(rden[:], all_ones[:], diagonal[:], start=True, stop=True)
 
         relu = [held.tile([P, S], F32, name=f"relu{b}") for b in range(BLOCKS)]
         means = held.tile([P, BLOCKS], F32, name="means")
-        weights = [held.tile([P, PIECE], F32, name=f"weights{k}", align_bytes=64) for k in range(PIECES)]
-
-        def spread(k, columns, step, func, scale):
-            repeated = held.tile([P, PIECE], F32, name=f"repeated{k}", align_bytes=64)
-            for first in range(0, PIECE, step):
-                entries = slice(first, first + step)
-                nc.scalar.activation(
-                    out=repeated[:, entries].rearrange("p (c f) -> p c f", f=SQ),
-                    in_=columns[:, first // SQ : (first + step) // SQ]
-                    .unsqueeze(2).to_broadcast([P, step // SQ, SQ]),
-                    func=func, scale=scale,
-                )
-                nc.vector.transpose(weights[k][:, entries], repeated[:, entries])
+        weights = [held.tile([P, PIECE], F32, name=f"weights{k}") for k in range(PIECES)]
 
         def relu_block(b):
             nc.scalar.activation(
-                out=relu[b][:], in_=raw[b][:], func=ACT.Relu, scale=1.0 / S,
+                out=relu[b][:], in_=raw[:, b, :], func=ACT.Relu, scale=1.0 / S,
                 accum_out=means[:, b : b + 1],
             )
 
         relu_block(0)
-        spread(0, columns0, PIECE // 2, ACT.Exp, 1.0)
         relu_block(1)
-        spread(1, columns1, PIECE, ACT.Copy, float(S))
+        for w in range(STEPS):
+            nc.scalar.activation(
+                out=weights[0][:, w * STEP : (w + 1) * STEP], in_=shifted[w][:], func=ACT.Exp
+            )
 
         squares = held.tile([P, BLOCKS], F32, name="squares")
         for b in range(BLOCKS):
@@ -148,6 +121,9 @@ def tile_tag_kernel(tc, h, gain, beta, att, offs, out):
                 out=centred_sq[:], in_=relu[b][:], func=ACT.Square,
                 scale=-float(S), bias=means[:, b : b + 1], accum_out=squares[:, b : b + 1],
             )
+        nc.scalar.activation(
+            out=weights[1][:], in_=weights_row[:], func=ACT.Copy, scale=float(S)
+        )
         var_eps = held.tile([P, BLOCKS], F32, name="var_eps")
         nc.scalar.activation(
             out=var_eps[:], in_=squares[:], func=ACT.Identity, scale=1.0 / S, bias=eps[:]
@@ -175,16 +151,16 @@ def tile_tag_kernel(tc, h, gain, beta, att, offs, out):
                 scale=minus_mean_gain[:, block], bias=betas[:, block],
             )
 
-        picked = held.tile([P, N // PIECE, BLOCKS, PIECE], F32, name="picked")
+        picked = held.tile([P, PIECES, BLOCKS, PIECE], F32, name="picked")
         unscaled = held.tile([P, BLOCKS, PIECE_TEAMS], F32, name="unscaled")
         pooled = held.tile([P, BLOCKS, T], F32, name="pooled")
 
-        def look_up(k, b):
+        def look_up(k, b, first, entries):
+            part = slice(first, first + entries)
+            listed = slice((k * PIECE + first) // 16, (k * PIECE + first + entries) // 16)
             nc.vector.tensor_tensor(
-                out=picked[:, k, b, :],
-                in0=relu[b][:].indirect(offsets[:, k * PIECE // 16 : (k + 1) * PIECE // 16]),
-                in1=weights[k][:],
-                op=ALU.mult,
+                out=picked[:, k, b, part], in0=relu[b][:].indirect(offsets[:, listed]),
+                in1=weights[k][:, part], op=ALU.mult,
             )
 
         def sum_teams(k, b):
@@ -193,18 +169,19 @@ def tile_tag_kernel(tc, h, gain, beta, att, offs, out):
                 out=sums, in_=picked[:, k, b, :].rearrange(BY_TEAM, l=L), axis=AXIS.X, op=ALU.add
             )
 
-        look_up(0, 0)
-        look_up(0, 1)
-        sum_teams(0, 0)
-        look_up(1, 0)
-        sum_teams(0, 1)
-        look_up(1, 1)
-        sum_teams(1, 0)
+        for w in range(STEPS):
+            for b in range(BLOCKS):
+                look_up(0, b, w * STEP, STEP)
+        for b in range(BLOCKS):
+            sum_teams(0, b)
+        for b in range(BLOCKS):
+            look_up(1, b, 0, PIECE)
         nc.vector.tensor_tensor(
             out=pooled[:, :, 0:PIECE_TEAMS], in0=unscaled[:],
             in1=rden[:].unsqueeze(1).to_broadcast([P, BLOCKS, PIECE_TEAMS]), op=ALU.mult,
         )
-        sum_teams(1, 1)
+        for b in range(BLOCKS):
+            sum_teams(1, b)
 
         result = held.tile([P, BLOCKS, T], F32, name="result")
         for b in range(BLOCKS):

@@ -62,23 +62,22 @@ def tile_tag_kernel(tc, h, gain, beta, att, offs, out):
             out=minus_top[:], in_=scores[:], axis=AXIS.X, op=ALU.max, negate=True
         )
 
-        def row_of(name, values, op, scalar, first, entries):
+        def own_columns(name, first, entries):
+            placed = held.tile([T, entries], F32, name=name)
+            by_team = placed[:].rearrange(BY_TEAM, l=L)
             teams = slice(first // L, (first + entries) // L)
-            shape = [T, entries // L, L]
-            placed = held.tile([T, entries], F32, name=f"placed_{name}")
-            nc.vector.scalar_tensor_tensor(
-                out=placed[:].rearrange(BY_TEAM, l=L),
-                in0=values[:].unsqueeze(1).to_broadcast(shape), scalar=scalar[:],
-                in1=identity[:, teams].unsqueeze(2).to_broadcast(shape),
-                op0=op, op1=ALU.mult,
-            )
-            row = psum.tile([P, entries], F32, name=f"row_{name}")
-            nc.tensor.matmul(row[:], all_ones[:], placed[:], start=True, stop=True)
-            return row
+            return placed, by_team, identity[:, teams].unsqueeze(2).to_broadcast(by_team.shape)
 
-        shifted = [
-            row_of(f"shifted{w}", scores, ALU.add, minus_top, w * STEP, STEP) for w in range(STEPS)
-        ]
+        shifted = []
+        for w in range(STEPS):
+            placed, by_team, own = own_columns(f"placed{w}", w * STEP, STEP)
+            nc.vector.scalar_tensor_tensor(
+                out=by_team, in0=scores[:].unsqueeze(1).to_broadcast(by_team.shape),
+                scalar=minus_top[:], in1=own, op0=ALU.add, op1=ALU.mult,
+            )
+            row = psum.tile([P, STEP], F32, name=f"shifted{w}")
+            nc.tensor.matmul(row[:], all_ones[:], placed[:], start=True, stop=True)
+            shifted.append(row)
 
         team_expd = held.tile([T, L], F32, name="team_expd")
         team_den = held.tile([T, 1], F32, name="team_den")
@@ -88,14 +87,16 @@ def tile_tag_kernel(tc, h, gain, beta, att, offs, out):
         )
         team_rden = held.tile([T, 1], F32, name="team_rden")
         nc.vector.reciprocal(out=team_rden[:], in_=team_den[:])
-        weights_row = row_of("weights", team_expd, ALU.mult, team_rden, PIECE, PIECE)
-        diagonal = held.tile([T, PIECE_TEAMS], F32, name="diagonal")
-        nc.vector.tensor_scalar(
-            out=diagonal[:], in0=identity[:, 0:PIECE_TEAMS], scalar1=team_rden[:],
-            scalar2=float(S), op0=ALU.mult, op1=ALU.mult,
+        rdens = team_rden[:].to_broadcast([T, P])
+        placed, by_team, own = own_columns("placed_e", PIECE, PIECE)
+        nc.vector.tensor_tensor(
+            out=by_team, in0=team_expd[:].unsqueeze(1).to_broadcast(by_team.shape), in1=own,
+            op=ALU.mult,
         )
+        weights_row = psum.tile([P, PIECE], F32, name="weights_row")
+        nc.tensor.matmul(weights_row[:], rdens, placed[:], start=True, stop=True)
         rden = psum.tile([P, PIECE_TEAMS], F32, name="rden")
-        nc.tensor.matmul(rden[:], all_ones[:], diagonal[:], start=True, stop=True)
+        nc.tensor.matmul(rden[:], rdens, identity[:, 0:PIECE_TEAMS], start=True, stop=True)
 
         relu = [held.tile([P, S], F32, name=f"relu{b}") for b in range(BLOCKS)]
         means = held.tile([P, BLOCKS], F32, name="means")
@@ -121,15 +122,15 @@ def tile_tag_kernel(tc, h, gain, beta, att, offs, out):
                 out=centred_sq[:], in_=relu[b][:], func=ACT.Square,
                 scale=-float(S), bias=means[:, b : b + 1], accum_out=squares[:, b : b + 1],
             )
-        nc.scalar.activation(
-            out=weights[1][:], in_=weights_row[:], func=ACT.Copy, scale=float(S)
-        )
         var_eps = held.tile([P, BLOCKS], F32, name="var_eps")
         nc.scalar.activation(
             out=var_eps[:], in_=squares[:], func=ACT.Identity, scale=1.0 / S, bias=eps[:]
         )
         rstd = held.tile([P, BLOCKS], F32, name="rstd")
         nc.gpsimd.tensor_tensor(out=rstd[:], in0=var_eps[:], in1=minus_half[:], op=ALU.pow)
+        nc.scalar.activation(
+            out=weights[1][:], in_=weights_row[:], func=ACT.Copy, scale=float(S)
+        )
         minus_means = held.tile([P, BLOCKS], F32, name="minus_means")
         nc.scalar.activation(out=minus_means[:], in_=means[:], func=ACT.Copy, scale=-1.0)
         minus_mean_gain = held.tile([P, BLOCKS], F32, name="minus_mean_gain")
@@ -176,9 +177,10 @@ def tile_tag_kernel(tc, h, gain, beta, att, offs, out):
             sum_teams(0, b)
         for b in range(BLOCKS):
             look_up(1, b, 0, PIECE)
-        nc.vector.tensor_tensor(
-            out=pooled[:, :, 0:PIECE_TEAMS], in0=unscaled[:],
-            in1=rden[:].unsqueeze(1).to_broadcast([P, BLOCKS, PIECE_TEAMS]), op=ALU.mult,
+        nc.vector.scalar_tensor_tensor(
+            out=pooled[:, :, 0:PIECE_TEAMS], in0=unscaled[:], scalar=float(S),
+            in1=rden[:].unsqueeze(1).to_broadcast([P, BLOCKS, PIECE_TEAMS]),
+            op0=ALU.mult, op1=ALU.mult,
         )
         for b in range(BLOCKS):
             sum_teams(1, b)

@@ -27,8 +27,9 @@ def tile_tag_kernel(tc, h, gain, beta, att, offs, out):
         offsets = held.tile([P, N // 16], U16, name="offsets")
         scores = held.tile([T, L], F32, name="scores")
         nc.sync.dma_start(scores[:], att.rearrange("o (t l) -> (o t) l", l=L))
-        raw = held.tile([P, BLOCKS, S], F32, name="raw")
-        nc.sync.dma_start(raw[:], h.rearrange("(p b) s -> p b s", b=BLOCKS))
+        raw = [held.tile([P, S], F32, name=f"raw{b}") for b in range(BLOCKS)]
+        for b, queue in enumerate((nc.scalar, nc.sync)):
+            queue.dma_start(raw[b][:], h.rearrange("(p b) s -> b p s", b=BLOCKS)[b])
         nc.sync.dma_start(offsets[:], offs)
         gains = held.tile([P, BLOCKS], F32, name="gains")
         betas = held.tile([P, BLOCKS], F32, name="betas")
@@ -39,8 +40,6 @@ def tile_tag_kernel(tc, h, gain, beta, att, offs, out):
         nc.gpsimd.memset(eps[:], EPS)
         all_ones = held.tile([T, P], F32, name="all_ones")
         nc.gpsimd.memset(all_ones[:], 1.0)
-        minus_half = held.tile([P, BLOCKS], F32, name="minus_half")
-        nc.gpsimd.memset(minus_half[:], -0.5)
         warm = held.tile([P, 1], F32, name="warm")
         nc.scalar.activation(out=warm[:], in_=eps[:], func=ACT.Exp)
         ones = held.tile([P, T], F32, name="ones")
@@ -104,33 +103,30 @@ def tile_tag_kernel(tc, h, gain, beta, att, offs, out):
 
         def relu_block(b):
             nc.scalar.activation(
-                out=relu[b][:], in_=raw[:, b, :], func=ACT.Relu, scale=1.0 / S,
+                out=relu[b][:], in_=raw[b][:], func=ACT.Relu, scale=1.0 / S,
                 accum_out=means[:, b : b + 1],
             )
 
-        relu_block(0)
-        relu_block(1)
-        for w in range(STEPS):
-            nc.scalar.activation(
-                out=weights[0][:, w * STEP : (w + 1) * STEP], in_=shifted[w][:], func=ACT.Exp
-            )
-
         squares = held.tile([P, BLOCKS], F32, name="squares")
-        for b in range(BLOCKS):
+
+        def squares_block(b):
             centred_sq = held.tile([P, S], F32, name=f"centred_sq{b}")
             nc.scalar.activation(
                 out=centred_sq[:], in_=relu[b][:], func=ACT.Square,
                 scale=-float(S), bias=means[:, b : b + 1], accum_out=squares[:, b : b + 1],
             )
-        var_eps = held.tile([P, BLOCKS], F32, name="var_eps")
-        nc.scalar.activation(
-            out=var_eps[:], in_=squares[:], func=ACT.Identity, scale=1.0 / S, bias=eps[:]
-        )
-        rstd = held.tile([P, BLOCKS], F32, name="rstd")
-        nc.gpsimd.tensor_tensor(out=rstd[:], in0=var_eps[:], in1=minus_half[:], op=ALU.pow)
-        nc.scalar.activation(
-            out=weights[1][:], in_=weights_row[:], func=ACT.Copy, scale=float(S)
-        )
+
+        def exp_step(w):
+            nc.scalar.activation(
+                out=weights[0][:, w * STEP : (w + 1) * STEP], in_=shifted[w][:], func=ACT.Exp
+            )
+
+        for b in range(BLOCKS):
+            relu_block(b)
+        for i in range(BLOCKS):
+            squares_block(i)
+            exp_step(i)
+
         minus_means = held.tile([P, BLOCKS], F32, name="minus_means")
         nc.scalar.activation(out=minus_means[:], in_=means[:], func=ACT.Copy, scale=-1.0)
         minus_mean_gain = held.tile([P, BLOCKS], F32, name="minus_mean_gain")
@@ -140,6 +136,13 @@ def tile_tag_kernel(tc, h, gain, beta, att, offs, out):
                 out=minus_mean_gain[:, block], in_=minus_means[:, block], func=ACT.Copy,
                 scale=gains[:, block],
             )
+        nc.scalar.activation(
+            out=weights[1][:], in_=weights_row[:], func=ACT.Copy, scale=float(S)
+        )
+        rstd = held.tile([P, BLOCKS], F32, name="rstd")
+        nc.scalar.activation(
+            out=rstd[:], in_=squares[:], func=ACT.Abs_reciprocal_sqrt, scale=1.0 / S, bias=eps[:]
+        )
         scale = held.tile([P, BLOCKS], F32, name="scale")
         shift = held.tile([P, BLOCKS], F32, name="shift")
         for b in range(BLOCKS):

@@ -92,8 +92,12 @@ def tile_tag_kernel(tc, h, gain, beta, att, offs, out):
             out=by_team, in0=team_expd[:].unsqueeze(1).to_broadcast(by_team.shape), in1=own,
             op=ALU.mult,
         )
-        weights_row = psum.tile([P, PIECE], F32, name="weights_row")
-        nc.tensor.matmul(weights_row[:], rdens, placed[:], start=True, stop=True)
+        weights_rows = [psum.tile([P, STEP], F32, name=f"weights_row{w}") for w in range(STEPS)]
+        for w in range(STEPS):
+            nc.tensor.matmul(
+                weights_rows[w][:], rdens, placed[:, w * STEP : (w + 1) * STEP],
+                start=True, stop=True,
+            )
         rden = psum.tile([P, PIECE_TEAMS], F32, name="rden")
         nc.tensor.matmul(rden[:], rdens, identity[:, 0:PIECE_TEAMS], start=True, stop=True)
 
@@ -136,9 +140,11 @@ def tile_tag_kernel(tc, h, gain, beta, att, offs, out):
                 out=minus_mean_gain[:, block], in_=minus_means[:, block], func=ACT.Copy,
                 scale=gains[:, block],
             )
-        nc.scalar.activation(
-            out=weights[1][:], in_=weights_row[:], func=ACT.Copy, scale=float(S)
-        )
+        for w in range(STEPS):
+            nc.scalar.activation(
+                out=weights[1][:, w * STEP : (w + 1) * STEP], in_=weights_rows[w][:],
+                func=ACT.Copy, scale=float(S),
+            )
         rstd = held.tile([P, BLOCKS], F32, name="rstd")
         nc.scalar.activation(
             out=rstd[:], in_=squares[:], func=ACT.Abs_reciprocal_sqrt, scale=1.0 / S, bias=eps[:]
@@ -178,8 +184,9 @@ def tile_tag_kernel(tc, h, gain, beta, att, offs, out):
                 look_up(0, b, w * STEP, STEP)
         for b in range(BLOCKS):
             sum_teams(0, b)
-        for b in range(BLOCKS):
-            look_up(1, b, 0, PIECE)
+        for w in range(STEPS):
+            for b in range(BLOCKS):
+                look_up(1, b, w * STEP, STEP)
         nc.vector.scalar_tensor_tensor(
             out=pooled[:, :, 0:PIECE_TEAMS], in0=unscaled[:], scalar=float(S),
             in1=rden[:].unsqueeze(1).to_broadcast([P, BLOCKS, PIECE_TEAMS]),

import concourse.mybir as mybir

F32 = mybir.dt.float32
U16 = mybir.dt.uint16
ALU = mybir.AluOpType
ACT = mybir.ActivationFunctionType
AXIS = mybir.AxisListType

P = 128
C, S, T, L, N = 256, 256, 32, 16, 512
EPS = 1e-5
BLOCKS = C // P
PIECE = S
PIECES = N // PIECE
PIECE_TEAMS = PIECE // L
STEP = PIECE // 2
STEPS = PIECE // STEP
BY_TEAM = "p (t l) -> p t l"


def tile_tag_kernel(tc, h, gain, beta, att, offs, out):
    nc = tc.nc
    with (
        tc.tile_pool(name="held", bufs=1) as held,
        tc.psum_pool(name="psum", bufs=1) as psum,
    ):
        offsets = held.tile([P, N // 16], U16, name="offsets")
        scores = held.tile([T, L], F32, name="scores")
        nc.sync.dma_start(scores[:], att.rearrange("o (t l) -> (o t) l", l=L))
        raw = [held.tile([P, S], F32, name=f"raw{b}") for b in range(BLOCKS)]
        for b, queue in enumerate((nc.scalar, nc.sync)):
            queue.dma_start(raw[b][:], h.rearrange("(p b) s -> b p s", b=BLOCKS)[b])
        nc.sync.dma_start(offsets[:], offs)
        gains = held.tile([P, BLOCKS], F32, name="gains")
        betas = held.tile([P, BLOCKS], F32, name="betas")
        nc.sync.dma_start(gains[:], gain.rearrange("(p b) o -> p (b o)", b=BLOCKS))
        nc.sync.dma_start(betas[:], beta.rearrange("(p b) o -> p (b o)", b=BLOCKS))

        eps = held.tile([P, 1], F32, name="eps")
        nc.gpsimd.memset(eps[:], EPS)
        all_ones = held.tile([T, P], F32, name="all_ones")
        nc.gpsimd.memset(all_ones[:], 1.0)
        warm = held.tile([P, 1], F32, name="warm")
        nc.scalar.activation(out=warm[:], in_=eps[:], func=ACT.Exp)
        ones = held.tile([P, T], F32, name="ones")
        nc.vector.memset(ones[:], 1.0)
        column = held.tile([P, T], F32, name="column", align_bytes=64)
        nc.vector.tensor_tensor_scan(
            column[:], ones[:], ones[:], -1.0, op0=ALU.mult, op1=ALU.add
        )
        partition = held.tile([P, T], F32, name="partition", align_bytes=64)
        nc.vector.transpose(partition[:], column[:])
        identity = held.tile([T, T], F32, name="identity")
        nc.vector.tensor_scalar(
            out=identity[:], in0=column[0:T, :], scalar1=partition[0:T, 0:1], scalar2=None,
            op0=ALU.is_equal,
        )

        minus_top = held.tile([T, 1], F32, name="minus_top")
        nc.vector.tensor_reduce(
            out=minus_top[:], in_=scores[:], axis=AXIS.X, op=ALU.max, negate=True
        )

        def own_columns(name, first, entries):
            placed = held.tile([T, entries], F32, name=name)
            by_team = placed[:].rearrange(BY_TEAM, l=L)
            teams = slice(first // L, (first + entries) // L)
            return placed, by_team, identity[:, teams].unsqueeze(2).to_broadcast(by_team.shape)

        shifted = []
        for w in range(STEPS):
            placed, by_team, own = own_columns(f"placed{w}", w * STEP, STEP)
            nc.vector.scalar_tensor_tensor(
                out=by_team, in0=scores[:].unsqueeze(1).to_broadcast(by_team.shape),
                scalar=minus_top[:], in1=own, op0=ALU.add, op1=ALU.mult,
            )
            row = psum.tile([P, STEP], F32, name=f"shifted{w}")
            nc.tensor.matmul(row[:], all_ones[:], placed[:], start=True, stop=True)
            shifted.append(row)

        team_expd = held.tile([T, L], F32, name="team_expd")
        team_den = held.tile([T, 1], F32, name="team_den")
        nc.scalar.activation(
            out=team_expd[:], in_=scores[:], func=ACT.Exp,
            bias=minus_top[:], accum_out=team_den[:],
        )
        team_rden = held.tile([T, 1], F32, name="team_rden")
        nc.vector.reciprocal(out=team_rden[:], in_=team_den[:])
        rdens = team_rden[:].to_broadcast([T, P])
        placed, by_team, own = own_columns("placed_e", PIECE, PIECE)
        nc.vector.tensor_tensor(
            out=by_team, in0=team_expd[:].unsqueeze(1).to_broadcast(by_team.shape), in1=own,
            op=ALU.mult,
        )
        weights_rows = [psum.tile([P, STEP], F32, name=f"weights_row{w}") for w in range(STEPS)]
        for w in range(STEPS):
            nc.tensor.matmul(
                weights_rows[w][:], rdens, placed[:, w * STEP : (w + 1) * STEP],
                start=True, stop=True,
            )
        rden = psum.tile([P, PIECE_TEAMS], F32, name="rden")
        nc.tensor.matmul(rden[:], rdens, identity[:, 0:PIECE_TEAMS], start=True, stop=True)

        relu = [held.tile([P, S], F32, name=f"relu{b}") for b in range(BLOCKS)]
        means = held.tile([P, BLOCKS], F32, name="means")
        weights = [held.tile([P, PIECE], F32, name=f"weights{k}") for k in range(PIECES)]

        def relu_block(b):
            nc.scalar.activation(
                out=relu[b][:], in_=raw[b][:], func=ACT.Relu, scale=1.0 / S,
                accum_out=means[:, b : b + 1],
            )

        squares = held.tile([P, BLOCKS], F32, name="squares")

        def squares_block(b):
            centred_sq = held.tile([P, S], F32, name=f"centred_sq{b}")
            nc.scalar.activation(
                out=centred_sq[:], in_=relu[b][:], func=ACT.Square,
                scale=-float(S), bias=means[:, b : b + 1], accum_out=squares[:, b : b + 1],
            )

        def exp_step(w):
            nc.scalar.activation(
                out=weights[0][:, w * STEP : (w + 1) * STEP], in_=shifted[w][:], func=ACT.Exp
            )

        for b in range(BLOCKS):
            relu_block(b)
        for i in range(BLOCKS):
            squares_block(i)
            exp_step(i)

        minus_means = held.tile([P, BLOCKS], F32, name="minus_means")
        nc.scalar.activation(out=minus_means[:], in_=means[:], func=ACT.Copy, scale=-1.0)
        minus_mean_gain = held.tile([P, BLOCKS], F32, name="minus_mean_gain")
        for b in range(BLOCKS):
            block = slice(b, b + 1)
            nc.scalar.activation(
                out=minus_mean_gain[:, block], in_=minus_means[:, block], func=ACT.Copy,
                scale=gains[:, block],
            )
        for w in range(STEPS):
            nc.scalar.activation(
                out=weights[1][:, w * STEP : (w + 1) * STEP], in_=weights_rows[w][:],
                func=ACT.Copy, scale=float(S),
            )
        rstd = held.tile([P, BLOCKS], F32, name="rstd")
        nc.scalar.activation(
            out=rstd[:], in_=squares[:], func=ACT.Abs_reciprocal_sqrt, scale=1.0 / S, bias=eps[:]
        )
        scale = held.tile([P, BLOCKS], F32, name="scale")
        shift = held.tile([P, BLOCKS], F32, name="shift")
        for b in range(BLOCKS):
            block = slice(b, b + 1)
            nc.scalar.activation(
                out=scale[:, block], in_=rstd[:, block], func=ACT.Copy, scale=gains[:, block]
            )
            nc.scalar.activation(
                out=shift[:, block], in_=rstd[:, block], func=ACT.Identity,
                scale=minus_mean_gain[:, block], bias=betas[:, block],
            )

        picked = held.tile([P, PIECES, BLOCKS, PIECE], F32, name="picked")
        unscaled = held.tile([P, BLOCKS, PIECE_TEAMS], F32, name="unscaled")
        pooled = held.tile([P, BLOCKS, T], F32, name="pooled")

        def look_up(k, b, first, entries):
            part = slice(first, first + entries)
            listed = slice((k * PIECE + first) // 16, (k * PIECE + first + entries) // 16)
            nc.vector.tensor_tensor(
                out=picked[:, k, b, part], in0=relu[b][:].indirect(offsets[:, listed]),
                in1=weights[k][:, part], op=ALU.mult,
            )

        def sum_teams(k, b):
            sums = unscaled[:, b, :] if k == 0 else pooled[:, b, PIECE_TEAMS:]
            nc.vector.tensor_reduce(
                out=sums, in_=picked[:, k, b, :].rearrange(BY_TEAM, l=L), axis=AXIS.X, op=ALU.add
            )

        for w in range(STEPS):
            for b in range(BLOCKS):
                look_up(0, b, w * STEP, STEP)
        for b in range(BLOCKS):
            sum_teams(0, b)
        for w in range(STEPS):
            for b in range(BLOCKS):
                look_up(1, b, w * STEP, STEP)
        nc.vector.scalar_tensor_tensor(
            out=pooled[:, :, 0:PIECE_TEAMS], in0=unscaled[:], scalar=float(S),
            in1=rden[:].unsqueeze(1).to_broadcast([P, BLOCKS, PIECE_TEAMS]),
            op0=ALU.mult, op1=ALU.mult,
        )
        for b in range(BLOCKS):
            sum_teams(1, b)

        result = held.tile([P, BLOCKS, T], F32, name="result")
        for b in range(BLOCKS):
            nc.vector.tensor_scalar(
                out=result[:, b, :], in0=pooled[:, b, :],
                scalar1=scale[:, b : b + 1], scalar2=shift[:, b : b + 1],
                op0=ALU.mult, op1=ALU.add,
            )
        nc.sync.dma_start(out.rearrange("(p b) t -> p b t", b=BLOCKS), result[:])
